import numpy as np
import ml_dtypes


def mxq(x, axis, fmt="e4m3"):
    dtype, down = {"e4m3": (ml_dtypes.float8_e4m3fn, 7), "e5m2": (ml_dtypes.float8_e5m2, 14)}[fmt]
    v = np.moveaxis(np.asarray(x, np.float32).astype(ml_dtypes.bfloat16).astype(np.float64), axis, -1)
    blocks = v.reshape(v.shape[:-1] + (-1, 32))
    amax = np.abs(blocks).max(-1, keepdims=True)
    byte = np.maximum(np.where(amax > 0, np.frexp(amax)[1] - 1 + 127, 0) - down, 1)
    scale = np.exp2(byte - 127.0)
    codes = (blocks / scale).astype(np.float32).astype(dtype).astype(np.float64)
    return np.moveaxis((codes * scale).reshape(v.shape), -1, axis)


WIDE = False


def mx_kscale(k):
    if not WIDE:
        return np.ones(k)
    levels = np.array([20, -20, 10, -10, 0])
    a = np.random.permutation(np.resize(levels, k // 512 * 4)).reshape(k // 512, 4)
    idx = np.arange(k)
    return np.exp2(a[idx // 512, idx % 128 // 32])


BF16 = ml_dtypes.bfloat16


def bf(x):
    return np.asarray(x, np.float32).astype(BF16)


def f64(x):
    return np.asarray(x).astype(np.float64)


B, HC, WC, C, F = 512, 2, 2, 512, 512


def preact(x_crop, W_r, W_i, b_r, b_i):
    sp = f64(x_crop)
    xr = sp[:, 0].transpose(1, 2, 0, 3)
    xi = sp[:, 1].transpose(1, 2, 0, 3)
    wr = f64(W_r)
    wi = f64(W_i)
    r = xr @ wr - xi @ wi + f64(b_r)
    i = xr @ wi + xi @ wr + f64(b_i)
    return np.stack([r.transpose(2, 0, 1, 3), i.transpose(2, 0, 1, 3)], axis=1)


def setup_inputs():
    u = mx_kscale(F)
    x_crop = bf(np.stack([np.random.standard_normal((B, HC, WC, C)), np.random.standard_normal((B, HC, WC, C))], axis=1))
    W_r0 = bf(np.random.standard_normal((HC, WC, C, F)) * 0.5 / np.sqrt(C))
    W_i0 = bf(np.random.standard_normal((HC, WC, C, F)) * 0.5 / np.sqrt(C))
    b_r = bf(np.random.standard_normal(F) * 0.3)
    b_i = bf(np.random.standard_normal(F) * 0.3)
    g = bf(np.random.standard_normal((B, 2, HC, WC, F)) * np.exp2(np.random.randint(-12, 1, (B, 1, HC, WC, 1))) * 8.0 * u)
    z = preact(x_crop, W_r0, W_i0, b_r, b_i)
    return {"x_crop": x_crop,
            "W_r": bf(f64(W_r0) / u),
            "W_i": bf(f64(W_i0) / u),
            "b_r": b_r,
            "b_i": b_i,
            "z": np.asarray(z, np.float32),
            "grad_out": g}


def reference(x_crop, W_r, W_i, b_r, b_i, z, grad_out):
    dz = f64(grad_out) * (f64(z) > 0.0)
    dr = mxq(dz[:, 0].transpose(1, 2, 0, 3), 3, "e5m2")
    di = mxq(dz[:, 1].transpose(1, 2, 0, 3), 3, "e5m2")
    wr = mxq(f64(W_r), 3, "e4m3").transpose(0, 1, 3, 2)
    wi = mxq(f64(W_i), 3, "e4m3").transpose(0, 1, 3, 2)
    rr = dr @ wr
    ii = di @ wi
    ri = dr @ wi
    ir = di @ wr
    gxr = rr + ii
    gxi = ir - ri
    return np.stack([gxr.transpose(2, 0, 1, 3), gxi.transpose(2, 0, 1, 3)], axis=1)

@@ -1,0 +1,155 @@
+from contextlib import ExitStack
+
+import concourse.mybir as mybir
+from concourse.masks import make_identity
+
+F32 = mybir.dt.float32
+BF16 = mybir.dt.bfloat16
+U32 = mybir.dt.uint32
+U8 = mybir.dt.uint8
+E4M3_X4 = mybir.dt.float8_e4m3fn_x4
+E5M2_X4 = mybir.dt.float8_e5m2_x4
+ALU = mybir.AluOpType
+
+P = 128
+PACK = 4
+BATCH, HEIGHT, WIDTH, CHANNELS, FEATURES = 512, 2, 2, 512, 512
+PIXELS = HEIGHT * WIDTH
+BATCH_TILES = BATCH // P
+PANEL_BLOCKS = 4
+PANEL_ROWS = PANEL_BLOCKS * P
+PAIRS = FEATURES // 2
+HALVES = PAIRS // P
+
+FLOPS = 2 * 4 * PIXELS * BATCH * CHANNELS * FEATURES
+BYTES = 2 * (2 * PIXELS * CHANNELS * FEATURES + 2 * PIXELS * BATCH * FEATURES) + 4 * (
+    2 * PIXELS * BATCH * FEATURES + 2 * PIXELS * BATCH * CHANNELS
+)
+
+
+def quantise_panel(nc, psum, stage, identity, panel, codes, scales, fp8_x4):
+    pairs = panel.bitcast(F32)
+    grouped = stage.tile([P, PANEL_BLOCKS, P, PACK], BF16, align_bytes=64)
+    grouped_pairs = grouped[:].bitcast(F32)
+    for first in range(0, PANEL_BLOCKS, 2):
+        bank = psum.tile([P, 2, HALVES, P], F32, tag="bank")
+        for i in range(2):
+            for half in range(HALVES):
+                nc.tensor.transpose(
+                    bank[:, i, half, :],
+                    pairs[:, first + i, half * P : (half + 1) * P],
+                    identity,
+                )
+        nc.scalar.copy(
+            out=grouped_pairs[:, first : first + 2, :, :],
+            in_=bank[:].rearrange("q i half row -> q i row half"),
+        )
+    nc.vector.quantize_mx(
+        out=codes.bitcast(fp8_x4),
+        scales=scales,
+        in_=grouped[:].rearrange("q block row t -> q (block row t)"),
+    )
+
+
+def tile_dot_pa_v_kernel(tc, x_crop, W_r, W_i, b_r, b_i, z, grad_out, out):
+    nc = tc.nc
+
+    g_rows = grad_out.rearrange("(t p) r h w f -> t p r h (w f)", p=P)
+    z_rows = z.rearrange("(t p) r h w f -> t p r h (w f)", p=P)
+    out_rows = out.rearrange("(t p) r h w c -> t p r h (w c)", p=P)
+    weight_rows = [
+        W.rearrange("h w (block p) f -> (h w) p block f", p=P) for W in (W_r, W_i)
+    ]
+
+    with ExitStack() as ctx:
+        const = ctx.enter_context(tc.tile_pool(name="const", bufs=1))
+        w_in = ctx.enter_context(tc.tile_pool(name="w_in", bufs=2 * PIXELS))
+        act_in = ctx.enter_context(tc.tile_pool(name="act_in", bufs=BATCH_TILES))
+        w_mx = ctx.enter_context(tc.tile_pool(name="w_mx", bufs=1))
+        stage = ctx.enter_context(tc.tile_pool(name="stage", bufs=3))
+        results = ctx.enter_context(tc.tile_pool(name="results", bufs=4))
+        psum = ctx.enter_context(tc.psum_pool(name="psum", bufs=8))
+
+        identity = const.tile([P, P], F32)
+        make_identity(nc, identity[:])
+
+        g_tiles, z_tiles, w_tiles = [], [], []
+
+        def load_batch_tile(t):
+            g_t = act_in.tile([P, 2, HEIGHT, WIDTH * FEATURES], BF16, name="g_t")
+            nc.sync.dma_start(out=g_t[:], in_=g_rows[t, :, :, :, :])
+            z_t = act_in.tile([P, 2, HEIGHT, WIDTH * FEATURES], F32, name="z_t")
+            nc.sync.dma_start(out=z_t[:], in_=z_rows[t, :, :, :, :])
+            g_tiles.append(g_t)
+            z_tiles.append(z_t)
+
+        load_batch_tile(0)
+        for pixel in range(PIXELS):
+            for part in range(2):
+                w_t = w_in.tile([P, PANEL_BLOCKS, FEATURES], BF16, name="w_t")
+                nc.sync.dma_start(out=w_t[:], in_=weight_rows[part][pixel, :, :, :])
+                w_tiles.append(w_t)
+        for t in range(1, BATCH_TILES):
+            load_batch_tile(t)
+
+        w_codes, w_scales = [], []
+        for unit in range(2 * PIXELS):
+            codes = w_mx.tile([P, PANEL_ROWS], U32, name="w_codes_%d" % unit, align_bytes=64)
+            scales = w_mx.tile([P, PANEL_ROWS], U8, name="w_scales_%d" % unit, align_bytes=64)
+            quantise_panel(
+                nc, psum, stage, identity[:], w_tiles[unit][:], codes[:], scales[:], E4M3_X4
+            )
+            w_codes.append(codes)
+            w_scales.append(scales)
+
+        for t in range(BATCH_TILES):
+            for h in range(HEIGHT):
+                dz = stage.tile([P, PANEL_BLOCKS, FEATURES], BF16)
+                nc.vector.scalar_tensor_tensor(
+                    out=dz[:].rearrange("p (r w) f -> p r (w f)", r=2),
+                    in0=z_tiles[t][:, :, h, :],
+                    scalar=0.0,
+                    in1=g_tiles[t][:, :, h, :],
+                    op0=ALU.is_gt,
+                    op1=ALU.mult,
+                )
+                d_codes = stage.tile([P, PANEL_ROWS], U32, align_bytes=64)
+                d_scales = stage.tile([P, PANEL_ROWS], U8, align_bytes=64)
+                quantise_panel(
+                    nc, psum, stage, identity[:], dz[:], d_codes[:], d_scales[:], E5M2_X4
+                )
+
+                result = results.tile([P, 2, WIDTH, CHANNELS], F32)
+                for w in range(WIDTH):
+                    pixel = h * WIDTH + w
+                    dr_cols = slice(w * P, (w + 1) * P)
+                    di_cols = slice((WIDTH + w) * P, (WIDTH + w + 1) * P)
+
+                    def product(acc, d_cols, part, start, stop):
+                        nc.tensor.matmul_mx(
+                            out=acc[:],
+                            lhsT=d_codes[:, d_cols].bitcast(E5M2_X4),
+                            lhsT_scale=d_scales[:, d_cols],
+                            rhs=w_codes[2 * pixel + part][:].bitcast(E4M3_X4),
+                            rhs_scale=w_scales[2 * pixel + part][:],
+                            start=start,
+                            stop=stop,
+                        )
+
+                    real = psum.tile([P, CHANNELS], F32, tag="bank")
+                    dr_wi = psum.tile([P, CHANNELS], F32, tag="bank")
+                    di_wr = psum.tile([P, CHANNELS], F32, tag="bank")
+                    product(real, dr_cols, 0, True, False)
+                    product(dr_wi, dr_cols, 1, True, True)
+                    product(real, di_cols, 1, False, True)
+                    product(di_wr, di_cols, 0, True, True)
+
+                    nc.scalar.copy(out=result[:, 0, w, :], in_=real[:])
+                    subtrahend = stage.tile([P, CHANNELS], F32)
+                    nc.scalar.copy(out=subtrahend[:], in_=dr_wi[:])
+                    nc.vector.tensor_tensor(
+                        out=result[:, 1, w, :], in0=di_wr[:], in1=subtrahend[:], op=ALU.subtract
+                    )
+                nc.sync.dma_start(
+                    out=out_rows[t, :, :, h, :], in_=result[:].rearrange("p r w c -> p r (w c)")
+                )

@@ -20,6 +20,7 @@ PANEL_BLOCKS = 4
 PANEL_ROWS = PANEL_BLOCKS * P
 PAIRS = FEATURES // 2
 HALVES = PAIRS // P
+ACT_BUFS = 3
 
 FLOPS = 2 * 4 * PIXELS * BATCH * CHANNELS * FEATURES
 BYTES = 2 * (2 * PIXELS * CHANNELS * FEATURES + 2 * PIXELS * BATCH * FEATURES) + 4 * (
@@ -32,17 +33,17 @@ def quantise_panel(nc, psum, stage, identity, panel, codes, scales, fp8_x4):
     grouped = stage.tile([P, PANEL_BLOCKS, P, PACK], BF16, align_bytes=64)
     grouped_pairs = grouped[:].bitcast(F32)
     for first in range(0, PANEL_BLOCKS, 2):
-        bank = psum.tile([P, 2, HALVES, P], F32, tag="bank")
+        transposed = psum.tile([P, 2, HALVES, P], F32)
         for i in range(2):
             for half in range(HALVES):
                 nc.tensor.transpose(
-                    bank[:, i, half, :],
+                    transposed[:, i, half, :],
                     pairs[:, first + i, half * P : (half + 1) * P],
                     identity,
                 )
         nc.scalar.copy(
             out=grouped_pairs[:, first : first + 2, :, :],
-            in_=bank[:].rearrange("q i half row -> q i row half"),
+            in_=transposed[:].rearrange("q i half row -> q i row half"),
         )
     nc.vector.quantize_mx(
         out=codes.bitcast(fp8_x4),
@@ -62,13 +63,14 @@ def tile_dot_pa_v_kernel(tc, x_crop, W_r, W_i, b_r, b_i, z, grad_out, out):
     ]
 
     with ExitStack() as ctx:
+        ctx.enter_context(tc.manual_schedule())
         const = ctx.enter_context(tc.tile_pool(name="const", bufs=1))
         w_in = ctx.enter_context(tc.tile_pool(name="w_in", bufs=2 * PIXELS))
-        act_in = ctx.enter_context(tc.tile_pool(name="act_in", bufs=BATCH_TILES))
+        act_in = ctx.enter_context(tc.tile_pool(name="act_in", bufs=ACT_BUFS))
         w_mx = ctx.enter_context(tc.tile_pool(name="w_mx", bufs=1))
         stage = ctx.enter_context(tc.tile_pool(name="stage", bufs=3))
-        results = ctx.enter_context(tc.tile_pool(name="results", bufs=4))
-        psum = ctx.enter_context(tc.psum_pool(name="psum", bufs=8))
+        results = ctx.enter_context(tc.tile_pool(name="results", bufs=6))
+        psum = ctx.enter_context(tc.psum_pool(name="psum", bufs=2))
 
         identity = const.tile([P, P], F32)
         make_identity(nc, identity[:])
@@ -89,8 +91,75 @@ def tile_dot_pa_v_kernel(tc, x_crop, W_r, W_i, b_r, b_i, z, grad_out, out):
                 w_t = w_in.tile([P, PANEL_BLOCKS, FEATURES], BF16, name="w_t")
                 nc.sync.dma_start(out=w_t[:], in_=weight_rows[part][pixel, :, :, :])
                 w_tiles.append(w_t)
-        for t in range(1, BATCH_TILES):
+        for t in range(1, ACT_BUFS):
             load_batch_tile(t)
+
+        dz_tiles, d_codes, d_scales = [], [], []
+
+        def mask(step):
+            t, h = divmod(step, HEIGHT)
+            dz = stage.tile([P, PANEL_BLOCKS, FEATURES], BF16, name="dz")
+            nc.vector.scalar_tensor_tensor(
+                out=dz[:].rearrange("p (r w) f -> p r (w f)", r=2),
+                in0=z_tiles[t][:, :, h, :],
+                scalar=0.0,
+                in1=g_tiles[t][:, :, h, :],
+                op0=ALU.is_gt,
+                op1=ALU.mult,
+            )
+            dz_tiles.append(dz)
+            if h == HEIGHT - 1 and t + ACT_BUFS < BATCH_TILES:
+                load_batch_tile(t + ACT_BUFS)
+
+        def quantise_dz(step):
+            codes = stage.tile([P, PANEL_ROWS], U32, name="d_codes", align_bytes=64)
+            scales = stage.tile([P, PANEL_ROWS], U8, name="d_scales", align_bytes=64)
+            quantise_panel(
+                nc, psum, stage, identity[:], dz_tiles[step][:], codes[:], scales[:], E5M2_X4
+            )
+            d_codes.append(codes)
+            d_scales.append(scales)
+
+        def multiply_and_store(step):
+            t, h = divmod(step, HEIGHT)
+            result = results.tile([P, 2, WIDTH, CHANNELS], F32, name="result")
+            for w in range(WIDTH):
+                pixel = h * WIDTH + w
+                dr_cols = slice(w * P, (w + 1) * P)
+                di_cols = slice((WIDTH + w) * P, (WIDTH + w + 1) * P)
+
+                def product(acc, d_cols, part, start, stop):
+                    nc.tensor.matmul_mx(
+                        out=acc[:],
+                        lhsT=d_codes[step][:, d_cols].bitcast(E5M2_X4),
+                        lhsT_scale=d_scales[step][:, d_cols],
+                        rhs=w_codes[2 * pixel + part][:].bitcast(E4M3_X4),
+                        rhs_scale=w_scales[2 * pixel + part][:],
+                        start=start,
+                        stop=stop,
+                    )
+
+                dr_wi = psum.tile([P, CHANNELS], F32, name="dr_wi")
+                real = psum.tile([P, CHANNELS], F32, name="real")
+                di_wr = psum.tile([P, CHANNELS], F32, name="di_wr")
+                product(dr_wi, dr_cols, 1, True, True)
+                product(real, dr_cols, 0, True, False)
+                product(real, di_cols, 1, False, True)
+                product(di_wr, di_cols, 0, True, True)
+
+                subtrahend = stage.tile([P, CHANNELS], F32, name="subtrahend")
+                nc.scalar.copy(out=subtrahend[:], in_=dr_wi[:])
+                nc.scalar.copy(out=result[:, 0, w, :], in_=real[:])
+                nc.vector.tensor_tensor(
+                    out=result[:, 1, w, :], in0=di_wr[:], in1=subtrahend[:], op=ALU.subtract
+                )
+            nc.sync.dma_start(
+                out=out_rows[t, :, :, h, :], in_=result[:].rearrange("p r w c -> p r (w c)")
+            )
+
+        mask(0)
+        mask(1)
+        quantise_dz(0)
 
         w_codes, w_scales = [], []
         for unit in range(2 * PIXELS):
@@ -102,54 +171,10 @@ def tile_dot_pa_v_kernel(tc, x_crop, W_r, W_i, b_r, b_i, z, grad_out, out):
             w_codes.append(codes)
             w_scales.append(scales)
 
-        for t in range(BATCH_TILES):
-            for h in range(HEIGHT):
-                dz = stage.tile([P, PANEL_BLOCKS, FEATURES], BF16)
-                nc.vector.scalar_tensor_tensor(
-                    out=dz[:].rearrange("p (r w) f -> p r (w f)", r=2),
-                    in0=z_tiles[t][:, :, h, :],
-                    scalar=0.0,
-                    in1=g_tiles[t][:, :, h, :],
-                    op0=ALU.is_gt,
-                    op1=ALU.mult,
-                )
-                d_codes = stage.tile([P, PANEL_ROWS], U32, align_bytes=64)
-                d_scales = stage.tile([P, PANEL_ROWS], U8, align_bytes=64)
-                quantise_panel(
-                    nc, psum, stage, identity[:], dz[:], d_codes[:], d_scales[:], E5M2_X4
-                )
-
-                result = results.tile([P, 2, WIDTH, CHANNELS], F32)
-                for w in range(WIDTH):
-                    pixel = h * WIDTH + w
-                    dr_cols = slice(w * P, (w + 1) * P)
-                    di_cols = slice((WIDTH + w) * P, (WIDTH + w + 1) * P)
-
-                    def product(acc, d_cols, part, start, stop):
-                        nc.tensor.matmul_mx(
-                            out=acc[:],
-                            lhsT=d_codes[:, d_cols].bitcast(E5M2_X4),
-                            lhsT_scale=d_scales[:, d_cols],
-                            rhs=w_codes[2 * pixel + part][:].bitcast(E4M3_X4),
-                            rhs_scale=w_scales[2 * pixel + part][:],
-                            start=start,
-                            stop=stop,
-                        )
-
-                    real = psum.tile([P, CHANNELS], F32, tag="bank")
-                    dr_wi = psum.tile([P, CHANNELS], F32, tag="bank")
-                    di_wr = psum.tile([P, CHANNELS], F32, tag="bank")
-                    product(real, dr_cols, 0, True, False)
-                    product(dr_wi, dr_cols, 1, True, True)
-                    product(real, di_cols, 1, False, True)
-                    product(di_wr, di_cols, 0, True, True)
-
-                    nc.scalar.copy(out=result[:, 0, w, :], in_=real[:])
-                    subtrahend = stage.tile([P, CHANNELS], F32)
-                    nc.scalar.copy(out=subtrahend[:], in_=dr_wi[:])
-                    nc.vector.tensor_tensor(
-                        out=result[:, 1, w, :], in0=di_wr[:], in1=subtrahend[:], op=ALU.subtract
-                    )
-                nc.sync.dma_start(
-                    out=out_rows[t, :, :, h, :], in_=result[:].rearrange("p r w c -> p r (w c)")
-                )
+        steps = BATCH_TILES * HEIGHT
+        for step in range(steps):
+            if step + 2 < steps:
+                mask(step + 2)
+            if step + 1 < steps:
+                quantise_dz(step + 1)
+            multiply_and_store(step)

@@ -33,7 +33,7 @@ def quantise_panel(nc, psum, stage, identity, panel, codes, scales, fp8_x4):
     grouped = stage.tile([P, PANEL_BLOCKS, P, PACK], BF16, align_bytes=64)
     grouped_pairs = grouped[:].bitcast(F32)
     for first in range(0, PANEL_BLOCKS, 2):
-        transposed = psum.tile([P, 2, HALVES, P], F32)
+        transposed = psum.tile([P, 2, HALVES, P], F32, tag="bank")
         for i in range(2):
             for half in range(HALVES):
                 nc.tensor.transpose(
@@ -70,29 +70,40 @@ def tile_dot_pa_v_kernel(tc, x_crop, W_r, W_i, b_r, b_i, z, grad_out, out):
         w_mx = ctx.enter_context(tc.tile_pool(name="w_mx", bufs=1))
         stage = ctx.enter_context(tc.tile_pool(name="stage", bufs=3))
         results = ctx.enter_context(tc.tile_pool(name="results", bufs=6))
-        psum = ctx.enter_context(tc.psum_pool(name="psum", bufs=2))
+        psum = ctx.enter_context(tc.psum_pool(name="psum", bufs=8))
 
         identity = const.tile([P, P], F32)
         make_identity(nc, identity[:])
 
         g_tiles, z_tiles, w_tiles = [], [], []
 
-        def load_batch_tile(t):
+        def load_batch_tile(t, pieces):
             g_t = act_in.tile([P, 2, HEIGHT, WIDTH * FEATURES], BF16, name="g_t")
-            nc.sync.dma_start(out=g_t[:], in_=g_rows[t, :, :, :, :])
             z_t = act_in.tile([P, 2, HEIGHT, WIDTH * FEATURES], F32, name="z_t")
-            nc.sync.dma_start(out=z_t[:], in_=z_rows[t, :, :, :, :])
             g_tiles.append(g_t)
             z_tiles.append(z_t)
+            rows = HEIGHT // pieces
+            for first in range(0, HEIGHT, rows):
+                nc.sync.dma_start(
+                    out=g_t[:, :, first : first + rows, :],
+                    in_=g_rows[t, :, :, first : first + rows, :],
+                )
+                nc.sync.dma_start(
+                    out=z_t[:, :, first : first + rows, :],
+                    in_=z_rows[t, :, :, first : first + rows, :],
+                )
+                if pieces > 1:
+                    load_weights(first)
 
-        load_batch_tile(0)
-        for pixel in range(PIXELS):
-            for part in range(2):
+        def load_weights(h):
+            for unit in range(2 * WIDTH * h, 2 * WIDTH * (h + 1)):
                 w_t = w_in.tile([P, PANEL_BLOCKS, FEATURES], BF16, name="w_t")
-                nc.sync.dma_start(out=w_t[:], in_=weight_rows[part][pixel, :, :, :])
+                nc.sync.dma_start(out=w_t[:], in_=weight_rows[unit % 2][unit // 2, :, :, :])
                 w_tiles.append(w_t)
+
+        load_batch_tile(0, HEIGHT)
         for t in range(1, ACT_BUFS):
-            load_batch_tile(t)
+            load_batch_tile(t, 1)
 
         dz_tiles, d_codes, d_scales = [], [], []
 
@@ -109,7 +120,7 @@ def tile_dot_pa_v_kernel(tc, x_crop, W_r, W_i, b_r, b_i, z, grad_out, out):
             )
             dz_tiles.append(dz)
             if h == HEIGHT - 1 and t + ACT_BUFS < BATCH_TILES:
-                load_batch_tile(t + ACT_BUFS)
+                load_batch_tile(t + ACT_BUFS, 1)
 
         def quantise_dz(step):
             codes = stage.tile([P, PANEL_ROWS], U32, name="d_codes", align_bytes=64)
@@ -139,9 +150,9 @@ def tile_dot_pa_v_kernel(tc, x_crop, W_r, W_i, b_r, b_i, z, grad_out, out):
                         stop=stop,
                     )
 
-                dr_wi = psum.tile([P, CHANNELS], F32, name="dr_wi")
-                real = psum.tile([P, CHANNELS], F32, name="real")
-                di_wr = psum.tile([P, CHANNELS], F32, name="di_wr")
+                dr_wi = psum.tile([P, CHANNELS], F32, name="dr_wi", tag="bank")
+                real = psum.tile([P, CHANNELS], F32, name="real", tag="bank")
+                di_wr = psum.tile([P, CHANNELS], F32, name="di_wr", tag="bank")
                 product(dr_wi, dr_cols, 1, True, True)
                 product(real, dr_cols, 0, True, False)
                 product(real, di_cols, 1, False, True)
@@ -157,22 +168,29 @@ def tile_dot_pa_v_kernel(tc, x_crop, W_r, W_i, b_r, b_i, z, grad_out, out):
                 out=out_rows[t, :, :, h, :], in_=result[:].rearrange("p r w c -> p r (w c)")
             )
 
-        mask(0)
-        mask(1)
-        quantise_dz(0)
+        def quantise_weights(h):
+            for unit in range(2 * WIDTH * h, 2 * WIDTH * (h + 1)):
+                codes = w_mx.tile([P, PANEL_ROWS], U32, name="w_codes_%d" % unit, align_bytes=64)
+                scales = w_mx.tile([P, PANEL_ROWS], U8, name="w_scales_%d" % unit, align_bytes=64)
+                quantise_panel(
+                    nc, psum, stage, identity[:], w_tiles[unit][:], codes[:], scales[:], E4M3_X4
+                )
+                w_codes.append(codes)
+                w_scales.append(scales)
 
         w_codes, w_scales = [], []
-        for unit in range(2 * PIXELS):
-            codes = w_mx.tile([P, PANEL_ROWS], U32, name="w_codes_%d" % unit, align_bytes=64)
-            scales = w_mx.tile([P, PANEL_ROWS], U8, name="w_scales_%d" % unit, align_bytes=64)
-            quantise_panel(
-                nc, psum, stage, identity[:], w_tiles[unit][:], codes[:], scales[:], E4M3_X4
-            )
-            w_codes.append(codes)
-            w_scales.append(scales)
-
         steps = BATCH_TILES * HEIGHT
-        for step in range(steps):
+
+        mask(0)
+        quantise_weights(0)
+        quantise_dz(0)
+        mask(1)
+        multiply_and_store(0)
+        quantise_weights(1)
+        quantise_dz(1)
+        mask(2)
+
+        for step in range(1, steps):
             if step + 2 < steps:
                 mask(step + 2)
             if step + 1 < steps:

@@ -16,11 +16,13 @@ PACK = 4
 BATCH, HEIGHT, WIDTH, CHANNELS, FEATURES = 512, 2, 2, 512, 512
 PIXELS = HEIGHT * WIDTH
 BATCH_TILES = BATCH // P
+STEPS = BATCH_TILES * HEIGHT
 PANEL_BLOCKS = 4
 PANEL_ROWS = PANEL_BLOCKS * P
 PAIRS = FEATURES // 2
 HALVES = PAIRS // P
 ACT_BUFS = 3
+W_R, W_I, MINUS_W_I = 0, 1, 2
 
 FLOPS = 2 * 4 * PIXELS * BATCH * CHANNELS * FEATURES
 BYTES = 2 * (2 * PIXELS * CHANNELS * FEATURES + 2 * PIXELS * BATCH * FEATURES) + 4 * (
@@ -28,9 +30,9 @@ BYTES = 2 * (2 * PIXELS * CHANNELS * FEATURES + 2 * PIXELS * BATCH * FEATURES) +
 )
 
 
-def quantise_panel(nc, psum, stage, identity, panel, codes, scales, fp8_x4):
+def transpose_panel(nc, psum, stage, identity, panel, rows_first):
     pairs = panel.bitcast(F32)
-    grouped = stage.tile([P, PANEL_BLOCKS, P, PACK], BF16, align_bytes=64)
+    grouped = stage.tile([P, PANEL_ROWS, PACK], BF16, align_bytes=64)
     grouped_pairs = grouped[:].bitcast(F32)
     for first in range(0, PANEL_BLOCKS, 2):
         transposed = psum.tile([P, 2, HALVES, P], F32, tag="bank")
@@ -41,14 +43,28 @@ def quantise_panel(nc, psum, stage, identity, panel, codes, scales, fp8_x4):
                     pairs[:, first + i, half * P : (half + 1) * P],
                     identity,
                 )
-        nc.scalar.copy(
-            out=grouped_pairs[:, first : first + 2, :, :],
-            in_=transposed[:].rearrange("q i half row -> q i row half"),
-        )
+        if rows_first:
+            nc.scalar.copy(
+                out=grouped_pairs.rearrange(
+                    "q (row block) half -> q row block half", block=PANEL_BLOCKS
+                )[:, :, first : first + 2, :],
+                in_=transposed[:].rearrange("q i half row -> q row i half"),
+            )
+        else:
+            nc.scalar.copy(
+                out=grouped_pairs.rearrange(
+                    "q (block row) half -> q block row half", block=PANEL_BLOCKS
+                )[:, first : first + 2, :, :],
+                in_=transposed[:].rearrange("q i half row -> q i row half"),
+            )
+    return grouped
+
+
+def quantise(nc, grouped, codes, scales, fp8_x4):
     nc.vector.quantize_mx(
-        out=codes.bitcast(fp8_x4),
-        scales=scales,
-        in_=grouped[:].rearrange("q block row t -> q (block row t)"),
+        out=codes[:].bitcast(fp8_x4),
+        scales=scales[:],
+        in_=grouped[:].rearrange("q column t -> q (column t)"),
     )
 
 
@@ -59,7 +75,7 @@ def tile_dot_pa_v_kernel(tc, x_crop, W_r, W_i, b_r, b_i, z, grad_out, out):
     z_rows = z.rearrange("(t p) r h w f -> t p r h (w f)", p=P)
     out_rows = out.rearrange("(t p) r h w c -> t p r h (w c)", p=P)
     weight_rows = [
-        W.rearrange("h w (block p) f -> (h w) p block f", p=P) for W in (W_r, W_i)
+        W.rearrange("h w (p block) f -> (h w) p block f", block=PANEL_BLOCKS) for W in (W_r, W_i)
     ]
 
     with ExitStack() as ctx:
@@ -77,23 +93,18 @@ def tile_dot_pa_v_kernel(tc, x_crop, W_r, W_i, b_r, b_i, z, grad_out, out):
 
         g_tiles, z_tiles, w_tiles = [], [], []
 
-        def load_batch_tile(t, pieces):
-            g_t = act_in.tile([P, 2, HEIGHT, WIDTH * FEATURES], BF16, name="g_t")
-            z_t = act_in.tile([P, 2, HEIGHT, WIDTH * FEATURES], F32, name="z_t")
-            g_tiles.append(g_t)
-            z_tiles.append(z_t)
-            rows = HEIGHT // pieces
-            for first in range(0, HEIGHT, rows):
-                nc.sync.dma_start(
-                    out=g_t[:, :, first : first + rows, :],
-                    in_=g_rows[t, :, :, first : first + rows, :],
-                )
-                nc.sync.dma_start(
-                    out=z_t[:, :, first : first + rows, :],
-                    in_=z_rows[t, :, :, first : first + rows, :],
-                )
-                if pieces > 1:
-                    load_weights(first)
+        def new_batch_tile():
+            g_tiles.append(act_in.tile([P, 2, HEIGHT, WIDTH * FEATURES], BF16, name="g_t"))
+            z_tiles.append(act_in.tile([P, 2, HEIGHT, WIDTH * FEATURES], F32, name="z_t"))
+
+        def load_image_rows(t, first, count):
+            rows = slice(first, first + count)
+            nc.sync.dma_start(out=g_tiles[t][:, :, rows, :], in_=g_rows[t, :, :, rows, :])
+            nc.sync.dma_start(out=z_tiles[t][:, :, rows, :], in_=z_rows[t, :, :, rows, :])
+
+        def load_batch_tile(t):
+            new_batch_tile()
+            load_image_rows(t, 0, HEIGHT)
 
         def load_weights(h):
             for unit in range(2 * WIDTH * h, 2 * WIDTH * (h + 1)):
@@ -101,9 +112,12 @@ def tile_dot_pa_v_kernel(tc, x_crop, W_r, W_i, b_r, b_i, z, grad_out, out):
                 nc.sync.dma_start(out=w_t[:], in_=weight_rows[unit % 2][unit // 2, :, :, :])
                 w_tiles.append(w_t)
 
-        load_batch_tile(0, HEIGHT)
+        new_batch_tile()
+        for h in range(HEIGHT):
+            load_image_rows(0, h, 1)
+            load_weights(h)
         for t in range(1, ACT_BUFS):
-            load_batch_tile(t, 1)
+            load_batch_tile(t)
 
         dz_tiles, d_codes, d_scales = [], [], []
 
@@ -120,16 +134,35 @@ def tile_dot_pa_v_kernel(tc, x_crop, W_r, W_i, b_r, b_i, z, grad_out, out):
             )
             dz_tiles.append(dz)
             if h == HEIGHT - 1 and t + ACT_BUFS < BATCH_TILES:
-                load_batch_tile(t + ACT_BUFS, 1)
+                load_batch_tile(t + ACT_BUFS)
 
         def quantise_dz(step):
+            grouped = transpose_panel(nc, psum, stage, identity[:], dz_tiles[step][:], False)
             codes = stage.tile([P, PANEL_ROWS], U32, name="d_codes", align_bytes=64)
             scales = stage.tile([P, PANEL_ROWS], U8, name="d_scales", align_bytes=64)
-            quantise_panel(
-                nc, psum, stage, identity[:], dz_tiles[step][:], codes[:], scales[:], E5M2_X4
-            )
+            quantise(nc, grouped, codes, scales, E5M2_X4)
             d_codes.append(codes)
             d_scales.append(scales)
+
+        w_codes, w_scales = {}, {}
+
+        def keep_weight(pixel, which, grouped):
+            label = "%d_%d" % (pixel, which)
+            codes = w_mx.tile([P, PANEL_ROWS], U32, name="w_codes_" + label, align_bytes=64)
+            scales = w_mx.tile([P, PANEL_ROWS], U8, name="w_scales_" + label, align_bytes=64)
+            quantise(nc, grouped, codes, scales, E4M3_X4)
+            w_codes[(pixel, which)] = codes
+            w_scales[(pixel, which)] = scales
+
+        def quantise_weights(h):
+            for pixel in range(WIDTH * h, WIDTH * (h + 1)):
+                w_r = transpose_panel(nc, psum, stage, identity[:], w_tiles[2 * pixel][:], True)
+                keep_weight(pixel, W_R, w_r)
+                w_i = transpose_panel(nc, psum, stage, identity[:], w_tiles[2 * pixel + 1][:], True)
+                minus_w_i = stage.tile([P, PANEL_ROWS, PACK], BF16, name="minus_w_i", align_bytes=64)
+                nc.vector.tensor_scalar_mul(out=minus_w_i[:], in0=w_i[:], scalar1=-1.0)
+                keep_weight(pixel, W_I, w_i)
+                keep_weight(pixel, MINUS_W_I, minus_w_i)
 
         def multiply_and_store(step):
             t, h = divmod(step, HEIGHT)
@@ -139,47 +172,32 @@ def tile_dot_pa_v_kernel(tc, x_crop, W_r, W_i, b_r, b_i, z, grad_out, out):
                 dr_cols = slice(w * P, (w + 1) * P)
                 di_cols = slice((WIDTH + w) * P, (WIDTH + w + 1) * P)
 
-                def product(acc, d_cols, part, start, stop):
+                def product(acc, d_cols, which, start, stop):
                     nc.tensor.matmul_mx(
                         out=acc[:],
                         lhsT=d_codes[step][:, d_cols].bitcast(E5M2_X4),
                         lhsT_scale=d_scales[step][:, d_cols],
-                        rhs=w_codes[2 * pixel + part][:].bitcast(E4M3_X4),
-                        rhs_scale=w_scales[2 * pixel + part][:],
+                        rhs=w_codes[(pixel, which)][:].bitcast(E4M3_X4),
+                        rhs_scale=w_scales[(pixel, which)][:],
                         start=start,
                         stop=stop,
                     )
 
-                dr_wi = psum.tile([P, CHANNELS], F32, name="dr_wi", tag="bank")
                 real = psum.tile([P, CHANNELS], F32, name="real", tag="bank")
-                di_wr = psum.tile([P, CHANNELS], F32, name="di_wr", tag="bank")
-                product(dr_wi, dr_cols, 1, True, True)
-                product(real, dr_cols, 0, True, False)
-                product(real, di_cols, 1, False, True)
-                product(di_wr, di_cols, 0, True, True)
+                imag = psum.tile([P, CHANNELS], F32, name="imag", tag="bank")
+                product(real, dr_cols, W_R, True, False)
+                product(imag, dr_cols, MINUS_W_I, True, False)
+                product(real, di_cols, W_I, False, True)
+                product(imag, di_cols, W_R, False, True)
 
-                subtrahend = stage.tile([P, CHANNELS], F32, name="subtrahend")
-                nc.scalar.copy(out=subtrahend[:], in_=dr_wi[:])
                 nc.scalar.copy(out=result[:, 0, w, :], in_=real[:])
-                nc.vector.tensor_tensor(
-                    out=result[:, 1, w, :], in0=di_wr[:], in1=subtrahend[:], op=ALU.subtract
-                )
+                if w == 0:
+                    nc.vector.tensor_copy(out=result[:, 1, w, :], in_=imag[:])
+                else:
+                    nc.scalar.copy(out=result[:, 1, w, :], in_=imag[:])
             nc.sync.dma_start(
                 out=out_rows[t, :, :, h, :], in_=result[:].rearrange("p r w c -> p r (w c)")
             )
-
-        def quantise_weights(h):
-            for unit in range(2 * WIDTH * h, 2 * WIDTH * (h + 1)):
-                codes = w_mx.tile([P, PANEL_ROWS], U32, name="w_codes_%d" % unit, align_bytes=64)
-                scales = w_mx.tile([P, PANEL_ROWS], U8, name="w_scales_%d" % unit, align_bytes=64)
-                quantise_panel(
-                    nc, psum, stage, identity[:], w_tiles[unit][:], codes[:], scales[:], E4M3_X4
-                )
-                w_codes.append(codes)
-                w_scales.append(scales)
-
-        w_codes, w_scales = [], []
-        steps = BATCH_TILES * HEIGHT
 
         mask(0)
         quantise_weights(0)
@@ -190,9 +208,9 @@ def tile_dot_pa_v_kernel(tc, x_crop, W_r, W_i, b_r, b_i, z, grad_out, out):
         quantise_dz(1)
         mask(2)
 
-        for step in range(1, steps):
-            if step + 2 < steps:
+        for step in range(1, STEPS):
+            if step + 2 < STEPS:
                 mask(step + 2)
-            if step + 1 < steps:
+            if step + 1 < STEPS:
                 quantise_dz(step + 1)
             multiply_and_store(step)

@@ -22,7 +22,6 @@ PANEL_ROWS = PANEL_BLOCKS * P
 PAIRS = FEATURES // 2
 HALVES = PAIRS // P
 ACT_BUFS = 3
-W_R, W_I, MINUS_W_I = 0, 1, 2
 
 FLOPS = 2 * 4 * PIXELS * BATCH * CHANNELS * FEATURES
 BYTES = 2 * (2 * PIXELS * CHANNELS * FEATURES + 2 * PIXELS * BATCH * FEATURES) + 4 * (
@@ -144,25 +143,16 @@ def tile_dot_pa_v_kernel(tc, x_crop, W_r, W_i, b_r, b_i, z, grad_out, out):
             d_codes.append(codes)
             d_scales.append(scales)
 
-        w_codes, w_scales = {}, {}
-
-        def keep_weight(pixel, which, grouped):
-            label = "%d_%d" % (pixel, which)
-            codes = w_mx.tile([P, PANEL_ROWS], U32, name="w_codes_" + label, align_bytes=64)
-            scales = w_mx.tile([P, PANEL_ROWS], U8, name="w_scales_" + label, align_bytes=64)
-            quantise(nc, grouped, codes, scales, E4M3_X4)
-            w_codes[(pixel, which)] = codes
-            w_scales[(pixel, which)] = scales
+        w_codes, w_scales = [], []
 
         def quantise_weights(h):
-            for pixel in range(WIDTH * h, WIDTH * (h + 1)):
-                w_r = transpose_panel(nc, psum, stage, identity[:], w_tiles[2 * pixel][:], True)
-                keep_weight(pixel, W_R, w_r)
-                w_i = transpose_panel(nc, psum, stage, identity[:], w_tiles[2 * pixel + 1][:], True)
-                minus_w_i = stage.tile([P, PANEL_ROWS, PACK], BF16, name="minus_w_i", align_bytes=64)
-                nc.vector.tensor_scalar_mul(out=minus_w_i[:], in0=w_i[:], scalar1=-1.0)
-                keep_weight(pixel, W_I, w_i)
-                keep_weight(pixel, MINUS_W_I, minus_w_i)
+            for unit in range(2 * WIDTH * h, 2 * WIDTH * (h + 1)):
+                grouped = transpose_panel(nc, psum, stage, identity[:], w_tiles[unit][:], True)
+                codes = w_mx.tile([P, PANEL_ROWS], U32, name="w_codes_%d" % unit, align_bytes=64)
+                scales = w_mx.tile([P, PANEL_ROWS], U8, name="w_scales_%d" % unit, align_bytes=64)
+                quantise(nc, grouped, codes, scales, E4M3_X4)
+                w_codes.append(codes)
+                w_scales.append(scales)
 
         def multiply_and_store(step):
             t, h = divmod(step, HEIGHT)
@@ -172,29 +162,31 @@ def tile_dot_pa_v_kernel(tc, x_crop, W_r, W_i, b_r, b_i, z, grad_out, out):
                 dr_cols = slice(w * P, (w + 1) * P)
                 di_cols = slice((WIDTH + w) * P, (WIDTH + w + 1) * P)
 
-                def product(acc, d_cols, which, start, stop):
+                def product(acc, d_cols, part, start, stop):
                     nc.tensor.matmul_mx(
                         out=acc[:],
                         lhsT=d_codes[step][:, d_cols].bitcast(E5M2_X4),
                         lhsT_scale=d_scales[step][:, d_cols],
-                        rhs=w_codes[(pixel, which)][:].bitcast(E4M3_X4),
-                        rhs_scale=w_scales[(pixel, which)][:],
+                        rhs=w_codes[2 * pixel + part][:].bitcast(E4M3_X4),
+                        rhs_scale=w_scales[2 * pixel + part][:],
                         start=start,
                         stop=stop,
                     )
 
+                dr_wi = psum.tile([P, CHANNELS], F32, name="dr_wi", tag="bank")
                 real = psum.tile([P, CHANNELS], F32, name="real", tag="bank")
-                imag = psum.tile([P, CHANNELS], F32, name="imag", tag="bank")
-                product(real, dr_cols, W_R, True, False)
-                product(imag, dr_cols, MINUS_W_I, True, False)
-                product(real, di_cols, W_I, False, True)
-                product(imag, di_cols, W_R, False, True)
+                di_wr = psum.tile([P, CHANNELS], F32, name="di_wr", tag="bank")
+                product(dr_wi, dr_cols, 1, True, True)
+                product(real, dr_cols, 0, True, False)
+                product(real, di_cols, 1, False, True)
+                product(di_wr, di_cols, 0, True, True)
 
+                subtrahend = stage.tile([P, CHANNELS], F32, name="subtrahend")
+                nc.scalar.copy(out=subtrahend[:], in_=dr_wi[:])
                 nc.scalar.copy(out=result[:, 0, w, :], in_=real[:])
-                if w == 0:
-                    nc.vector.tensor_copy(out=result[:, 1, w, :], in_=imag[:])
-                else:
-                    nc.scalar.copy(out=result[:, 1, w, :], in_=imag[:])
+                nc.vector.tensor_tensor(
+                    out=result[:, 1, w, :], in0=di_wr[:], in1=subtrahend[:], op=ALU.subtract
+                )
             nc.sync.dma_start(
                 out=out_rows[t, :, :, h, :], in_=result[:].rearrange("p r w c -> p r (w c)")
             )

from contextlib import ExitStack

import concourse.mybir as mybir
from concourse.masks import make_identity

F32 = mybir.dt.float32
BF16 = mybir.dt.bfloat16
U32 = mybir.dt.uint32
U8 = mybir.dt.uint8
E4M3_X4 = mybir.dt.float8_e4m3fn_x4
E5M2_X4 = mybir.dt.float8_e5m2_x4
ALU = mybir.AluOpType

P = 128
PACK = 4
BATCH, HEIGHT, WIDTH, CHANNELS, FEATURES = 512, 2, 2, 512, 512
PIXELS = HEIGHT * WIDTH
BATCH_TILES = BATCH // P
STEPS = BATCH_TILES * HEIGHT
PANEL_BLOCKS = 4
PANEL_ROWS = PANEL_BLOCKS * P
PAIRS = FEATURES // 2
HALVES = PAIRS // P
ACT_BUFS = 3

FLOPS = 2 * 4 * PIXELS * BATCH * CHANNELS * FEATURES
BYTES = 2 * (2 * PIXELS * CHANNELS * FEATURES + 2 * PIXELS * BATCH * FEATURES) + 4 * (
    2 * PIXELS * BATCH * FEATURES + 2 * PIXELS * BATCH * CHANNELS
)


def transpose_panel(nc, psum, stage, identity, panel, rows_first):
    pairs = panel.bitcast(F32)
    grouped = stage.tile([P, PANEL_ROWS, PACK], BF16, align_bytes=64)
    grouped_pairs = grouped[:].bitcast(F32)
    for first in range(0, PANEL_BLOCKS, 2):
        transposed = psum.tile([P, 2, HALVES, P], F32, tag="bank")
        for i in range(2):
            for half in range(HALVES):
                nc.tensor.transpose(
                    transposed[:, i, half, :],
                    pairs[:, first + i, half * P : (half + 1) * P],
                    identity,
                )
        if rows_first:
            nc.scalar.copy(
                out=grouped_pairs.rearrange(
                    "q (row block) half -> q row block half", block=PANEL_BLOCKS
                )[:, :, first : first + 2, :],
                in_=transposed[:].rearrange("q i half row -> q row i half"),
            )
        else:
            nc.scalar.copy(
                out=grouped_pairs.rearrange(
                    "q (block row) half -> q block row half", block=PANEL_BLOCKS
                )[:, first : first + 2, :, :],
                in_=transposed[:].rearrange("q i half row -> q i row half"),
            )
    return grouped


def quantise(nc, grouped, codes, scales, fp8_x4):
    nc.vector.quantize_mx(
        out=codes[:].bitcast(fp8_x4),
        scales=scales[:],
        in_=grouped[:].rearrange("q column t -> q (column t)"),
    )


def tile_dot_pa_v_kernel(tc, x_crop, W_r, W_i, b_r, b_i, z, grad_out, out):
    nc = tc.nc

    g_rows = grad_out.rearrange("(t p) r h w f -> t p r h (w f)", p=P)
    z_rows = z.rearrange("(t p) r h w f -> t p r h (w f)", p=P)
    out_rows = out.rearrange("(t p) r h w c -> t p r h (w c)", p=P)
    weight_rows = [
        W.rearrange("h w (p block) f -> (h w) p block f", block=PANEL_BLOCKS) for W in (W_r, W_i)
    ]

    with ExitStack() as ctx:
        ctx.enter_context(tc.manual_schedule())
        const = ctx.enter_context(tc.tile_pool(name="const", bufs=1))
        w_in = ctx.enter_context(tc.tile_pool(name="w_in", bufs=2 * PIXELS))
        act_in = ctx.enter_context(tc.tile_pool(name="act_in", bufs=ACT_BUFS))
        w_mx = ctx.enter_context(tc.tile_pool(name="w_mx", bufs=1))
        stage = ctx.enter_context(tc.tile_pool(name="stage", bufs=3))
        results = ctx.enter_context(tc.tile_pool(name="results", bufs=6))
        psum = ctx.enter_context(tc.psum_pool(name="psum", bufs=8))

        identity = const.tile([P, P], F32)
        make_identity(nc, identity[:])

        g_tiles, z_tiles, w_tiles = [], [], []

        def new_batch_tile():
            g_tiles.append(act_in.tile([P, 2, HEIGHT, WIDTH * FEATURES], BF16, name="g_t"))
            z_tiles.append(act_in.tile([P, 2, HEIGHT, WIDTH * FEATURES], F32, name="z_t"))

        def load_image_rows(t, first, count):
            rows = slice(first, first + count)
            nc.sync.dma_start(out=g_tiles[t][:, :, rows, :], in_=g_rows[t, :, :, rows, :])
            nc.sync.dma_start(out=z_tiles[t][:, :, rows, :], in_=z_rows[t, :, :, rows, :])

        def load_batch_tile(t):
            new_batch_tile()
            load_image_rows(t, 0, HEIGHT)

        def load_weights(h):
            for unit in range(2 * WIDTH * h, 2 * WIDTH * (h + 1)):
                w_t = w_in.tile([P, PANEL_BLOCKS, FEATURES], BF16, name="w_t")
                nc.sync.dma_start(out=w_t[:], in_=weight_rows[unit % 2][unit // 2, :, :, :])
                w_tiles.append(w_t)

        new_batch_tile()
        for h in range(HEIGHT):
            load_image_rows(0, h, 1)
            load_weights(h)
        for t in range(1, ACT_BUFS):
            load_batch_tile(t)

        dz_tiles, d_codes, d_scales = [], [], []

        def mask(step):
            t, h = divmod(step, HEIGHT)
            dz = stage.tile([P, PANEL_BLOCKS, FEATURES], BF16, name="dz")
            nc.vector.scalar_tensor_tensor(
                out=dz[:].rearrange("p (r w) f -> p r (w f)", r=2),
                in0=z_tiles[t][:, :, h, :],
                scalar=0.0,
                in1=g_tiles[t][:, :, h, :],
                op0=ALU.is_gt,
                op1=ALU.mult,
            )
            dz_tiles.append(dz)
            if h == HEIGHT - 1 and t + ACT_BUFS < BATCH_TILES:
                load_batch_tile(t + ACT_BUFS)

        def quantise_dz(step):
            grouped = transpose_panel(nc, psum, stage, identity[:], dz_tiles[step][:], False)
            codes = stage.tile([P, PANEL_ROWS], U32, name="d_codes", align_bytes=64)
            scales = stage.tile([P, PANEL_ROWS], U8, name="d_scales", align_bytes=64)
            quantise(nc, grouped, codes, scales, E5M2_X4)
            d_codes.append(codes)
            d_scales.append(scales)

        w_codes, w_scales = [], []

        def quantise_weights(h):
            for unit in range(2 * WIDTH * h, 2 * WIDTH * (h + 1)):
                grouped = transpose_panel(nc, psum, stage, identity[:], w_tiles[unit][:], True)
                codes = w_mx.tile([P, PANEL_ROWS], U32, name="w_codes_%d" % unit, align_bytes=64)
                scales = w_mx.tile([P, PANEL_ROWS], U8, name="w_scales_%d" % unit, align_bytes=64)
                quantise(nc, grouped, codes, scales, E4M3_X4)
                w_codes.append(codes)
                w_scales.append(scales)

        def multiply_and_store(step):
            t, h = divmod(step, HEIGHT)
            result = results.tile([P, 2, WIDTH, CHANNELS], F32, name="result")
            for w in range(WIDTH):
                pixel = h * WIDTH + w
                dr_cols = slice(w * P, (w + 1) * P)
                di_cols = slice((WIDTH + w) * P, (WIDTH + w + 1) * P)

                def product(acc, d_cols, part, start, stop):
                    nc.tensor.matmul_mx(
                        out=acc[:],
                        lhsT=d_codes[step][:, d_cols].bitcast(E5M2_X4),
                        lhsT_scale=d_scales[step][:, d_cols],
                        rhs=w_codes[2 * pixel + part][:].bitcast(E4M3_X4),
                        rhs_scale=w_scales[2 * pixel + part][:],
                        start=start,
                        stop=stop,
                    )

                dr_wi = psum.tile([P, CHANNELS], F32, name="dr_wi", tag="bank")
                real = psum.tile([P, CHANNELS], F32, name="real", tag="bank")
                di_wr = psum.tile([P, CHANNELS], F32, name="di_wr", tag="bank")
                product(dr_wi, dr_cols, 1, True, True)
                product(real, dr_cols, 0, True, False)
                product(real, di_cols, 1, False, True)
                product(di_wr, di_cols, 0, True, True)

                subtrahend = stage.tile([P, CHANNELS], F32, name="subtrahend")
                nc.scalar.copy(out=subtrahend[:], in_=dr_wi[:])
                nc.scalar.copy(out=result[:, 0, w, :], in_=real[:])
                nc.vector.tensor_tensor(
                    out=result[:, 1, w, :], in0=di_wr[:], in1=subtrahend[:], op=ALU.subtract
                )
            nc.sync.dma_start(
                out=out_rows[t, :, :, h, :], in_=result[:].rearrange("p r w c -> p r (w c)")
            )

        mask(0)
        quantise_weights(0)
        quantise_dz(0)
        mask(1)
        multiply_and_store(0)
        quantise_weights(1)
        quantise_dz(1)
        mask(2)

        for step in range(1, STEPS):
            if step + 2 < STEPS:
                mask(step + 2)
            if step + 1 < STEPS:
                quantise_dz(step + 1)
            multiply_and_store(step)
